import numpy as np
import ml_dtypes


def mxq(x, axis, fmt="e4m3"):
    dtype, down = {"e4m3": (ml_dtypes.float8_e4m3fn, 7), "e5m2": (ml_dtypes.float8_e5m2, 14)}[fmt]
    v = np.moveaxis(np.asarray(x, np.float32).astype(ml_dtypes.bfloat16).astype(np.float64), axis, -1)
    blocks = v.reshape(v.shape[:-1] + (-1, 32))
    amax = np.abs(blocks).max(-1, keepdims=True)
    byte = np.maximum(np.where(amax > 0, np.frexp(amax)[1] - 1 + 127, 0) - down, 1)
    scale = np.exp2(byte - 127.0)
    codes = (blocks / scale).astype(np.float32).astype(dtype).astype(np.float64)
    return np.moveaxis((codes * scale).reshape(v.shape), -1, axis)


WIDE = False


def mx_kscale(k):
    if not WIDE:
        return np.ones(k)
    levels = np.array([30, -30])
    if k % 512:
        return np.exp2(np.random.permutation(np.resize(levels, k // 32))).repeat(32)
    a = np.empty((k // 512, 16))
    for p in range(k // 512):
        a[p, :8] = np.random.permutation(np.resize(levels, 8))
        for g in range(8):
            far = levels[np.abs(levels - a[p, g]) >= 10]
            a[p, g + 8] = far[np.random.randint(len(far))]
    return np.exp2(a.ravel()).repeat(32)


BF16 = ml_dtypes.bfloat16


def bf(x):
    return np.asarray(x, np.float32).astype(BF16)


def f64(x):
    return np.asarray(x).astype(np.float64)


N, T, C, D, H, DO = 4, 256, 1024, 1024, 16, 1024
HD = D // H


def head_scores(q, k):
    return np.stack([(q * k[:, :, g:g + 1, :]).sum(-1) for g in range(H)], axis=-1)


def setup_inputs():
    s = mx_kscale(C)
    return {"x": bf(np.random.standard_normal((N, T, C)) * s),
            "w_qk": bf(np.random.standard_normal((C, 2 * D)) / np.sqrt(C) / s[:, None]),
            "b_qk": bf(np.random.standard_normal(2 * D) * 0.3)}


def reference(x, w_qk, b_qk):
    qk = (mxq(f64(x), 2, "e5m2") @ mxq(f64(w_qk), 0, "e4m3")) + f64(b_qk)
    qk = qk.reshape(N, T, 2, H, HD)
    q, k = qk[:, :, 0], qk[:, :, 1]
    s = head_scores(q * HD ** -0.5, k)
    e = np.exp(s - s.max(-1, keepdims=True))
    return e / e.sum(-1, keepdims=True)

@@ -1,0 +1,329 @@
+from contextlib import ExitStack
+
+import concourse.mybir as mybir
+from concourse.masks import make_identity
+
+F32 = mybir.dt.float32
+BF16 = mybir.dt.bfloat16
+U32 = mybir.dt.uint32
+U8 = mybir.dt.uint8
+E4M3X4 = mybir.dt.float8_e4m3fn_x4
+E5M2X4 = mybir.dt.float8_e5m2_x4
+ALU = mybir.AluOpType
+ACT = mybir.ActivationFunctionType
+AX = mybir.AxisListType
+
+TOKENS, C, D, H = 1024, 1024, 1024, 16
+HD = D // H
+P = 128
+HALF = P // 2
+QUAD = P // 4
+PACK = 4
+K_PASS = P * PACK
+PASSES = C // K_PASS
+BANK = 512
+BLOCKS = 2 * D // BANK
+Q_BLOCKS = BLOCKS // 2
+HEADS_PER_BLOCK = BANK // HD
+TILES = TOKENS // P
+PAIRS = TILES // 2
+CHUNKS = BLOCKS * PASSES
+GROUPS = QUAD
+GROUPS_PER_BANK = 8
+PSUM_BANKS = 8
+
+FLOPS = 2 * TOKENS * C * 2 * D + 2 * TOKENS * H * H * HD
+
+
+def tile_attention_pa_kernel(tc, x, w_qk, b_qk, out):
+    nc = tc.nc
+    x_rows = x.rearrange("n t c -> (n t) c")
+    out_rows = out.rearrange("n t h g -> (n t) (h g)")
+
+    with ExitStack() as ctx:
+        keep = ctx.enter_context(tc.tile_pool(name="keep", bufs=1))
+        stage = ctx.enter_context(tc.tile_pool(name="stage", bufs=2))
+        psum = ctx.enter_context(tc.psum_pool(name="psum", bufs=1))
+        ctx.enter_context(tc.manual_schedule())
+
+        banks_taken = []
+
+        def next_bank():
+            index = len(banks_taken) % PSUM_BANKS
+            bank = psum.tile([P, BANK], F32, name="bank%d" % index)
+            banks_taken.append(index)
+            return bank
+
+        ident = keep.tile([P, P], F32, name="ident")
+        x_raw = [keep.tile([P, C], BF16, name="x_raw%d" % t) for t in range(TILES)]
+        w_raw = [keep.tile([P, PACK, BANK], BF16, name="w_raw%d" % c) for c in range(CHUNKS)]
+        x_codes = [keep.tile([P, PASSES * P], U32, name="x_codes%d" % t, align_bytes=64) for t in range(TILES)]
+        x_scales = [keep.tile([P, PASSES * P], U8, name="x_scales%d" % t, align_bytes=64) for t in range(TILES)]
+        w_codes = [keep.tile([P, BANK], U32, name="w_codes%d" % c, align_bytes=64) for c in range(CHUNKS)]
+        w_scales = [keep.tile([P, BANK], U8, name="w_scales%d" % c, align_bytes=64) for c in range(CHUNKS)]
+        proj = [[keep.tile([P, HEADS_PER_BLOCK, 2, HD], F32, name="proj%d_%d" % (r, b)) for b in range(BLOCKS)]
+                for r in range(PAIRS)]
+        k_masked = [keep.tile([P, GROUPS, 4, 2, H], F32, name="k_masked%d" % i) for i in range(2)]
+        k_bias = keep.tile([P, D], BF16, name="k_bias")
+        q_bias_rows = keep.tile([P, 2, HD], BF16, name="q_bias_rows")
+        q_bias_rows32 = keep.tile([P, 2 * HD], F32, name="q_bias_rows32")
+        q_bias = keep.tile([P, H], F32, name="q_bias")
+        x_grouped, w_grouped, x_bank, mx_bank = {}, {}, {}, {}
+        q_moving, scores, t_bank, s_bank, soft = {}, {}, {}, {}, {}
+
+        def load_x(t):
+            nc.sync.dma_start(out=x_raw[t][:], in_=x_rows[t * P:(t + 1) * P, :])
+
+        def load_w(c):
+            b, g = divmod(c, PASSES)
+            rows = w_qk[g * K_PASS:(g + 1) * K_PASS, b * BANK:(b + 1) * BANK]
+            nc.sync.dma_start(out=w_raw[c][:], in_=rows.rearrange("(p j) n -> p j n", j=PACK))
+
+        def transpose_x(t):
+            words = x_raw[t][:].bitcast(F32)
+            bank = next_bank()
+            x_bank[t] = bank
+            for g in range(PASSES):
+                for u in range(2):
+                    slot = 2 * g + u
+                    nc.tensor.transpose(bank[:, slot * P:(slot + 1) * P],
+                                        words[:, 2 * P * g + u:2 * P * (g + 1):2], ident[:])
+
+        def empty_x(t):
+            grouped = stage.tile([P, PASSES * P * PACK], BF16, name="x_grouped", bufs=4, align_bytes=64)
+            x_grouped[t] = grouped
+            nc.scalar.copy(out=grouped[:].bitcast(F32).rearrange("p (g r u) -> p g r u", g=PASSES, u=2),
+                           in_=x_bank[t][:].rearrange("p (g u r) -> p g r u", g=PASSES, u=2))
+
+        def quantize_x(t):
+            nc.vector.quantize_mx(out=x_codes[t][:].bitcast(E5M2X4), scales=x_scales[t][:], in_=x_grouped[t][:])
+
+        def interleave_w(c, copy):
+            grouped = stage.tile([P, BANK * PACK], BF16, name="w_grouped", bufs=3, align_bytes=64)
+            w_grouped[c] = grouped
+            copy(out=grouped[:].rearrange("p (c i t) -> p c t i", i=4, t=PACK),
+                 in_=w_raw[c][:].rearrange("p t (c i) -> p c t i", i=4))
+
+        def quantize_w(c):
+            nc.vector.quantize_mx(out=w_codes[c][:].bitcast(E4M3X4), scales=w_scales[c][:], in_=w_grouped[c][:])
+
+        def project(t, b):
+            bank = next_bank()
+            for g in range(PASSES):
+                c = b * PASSES + g
+                nc.tensor.matmul_mx(
+                    out=bank[:],
+                    lhsT=x_codes[t][:, g * P:(g + 1) * P].bitcast(E5M2X4),
+                    lhsT_scale=x_scales[t][:, g * P:(g + 1) * P],
+                    rhs=w_codes[c][:].bitcast(E4M3X4),
+                    rhs_scale=w_scales[c][:],
+                    start=(g == 0), stop=(g == PASSES - 1))
+            mx_bank[t, b] = bank
+
+        def empty_projection(t, b):
+            r, a = divmod(t, 2)
+            src = mx_bank[t, b][:].rearrange("p (h d) -> p h d", d=HD)
+            dst = proj[r][b][:, :, a, :]
+            if b < Q_BLOCKS:
+                nc.scalar.copy(out=dst, in_=src)
+            else:
+                cols = slice((b - Q_BLOCKS) * BANK, (b - Q_BLOCKS + 1) * BANK)
+                nc.vector.tensor_tensor(out=dst, in0=src, in1=k_bias[:, cols].rearrange("p (h d) -> p h d", d=HD),
+                                        op=ALU.add)
+
+        def transpose_heads(r, s):
+            bank = next_bank()
+            b, first = divmod(4 * s, HEADS_PER_BLOCK)
+            for i in range(4):
+                nc.tensor.transpose(bank[:, i * P:(i + 1) * P],
+                                    proj[r][b][:, first + i, :, :].rearrange("p a d -> p (a d)"), ident[:])
+            t_bank[r, s] = bank
+
+        def empty_heads(r, s):
+            src = t_bank[r, s][:].rearrange("p (h j m) -> p m j h", h=4, j=4)
+            if s < 4:
+                if s == 0:
+                    q_moving[r] = stage.tile([P, GROUPS, 4, H], F32, name="q_moving")
+                bias = q_bias[:, 4 * s:4 * s + 4].unsqueeze(1).unsqueeze(1).to_broadcast([P, GROUPS, 4, 4])
+                nc.vector.tensor_tensor(out=q_moving[r][:, :, :, 4 * s:4 * s + 4], in0=src, in1=bias, op=ALU.add)
+            else:
+                g0 = 4 * (s - 4)
+                for a in range(2):
+                    rows = slice(a * HALF, (a + 1) * HALF)
+                    nc.scalar.copy(out=k_masked[r % 2][rows, :, :, a, g0:g0 + 4], in_=src[rows])
+
+        def score(r, s):
+            bank = next_bank()
+            for i in range(GROUPS_PER_BANK):
+                m = s * GROUPS_PER_BANK + i
+                nc.tensor.matmul(bank[:, i * 4 * H:(i + 1) * 4 * H],
+                                 lhsT=k_masked[r % 2][:, m].rearrange("p j a g -> p (j a g)"),
+                                 rhs=q_moving[r][:, m].rearrange("p j h -> p (j h)"),
+                                 start=True, stop=True)
+            s_bank[r, s] = bank
+
+        def empty_scores(r, s):
+            if s == 0:
+                scores[r] = stage.tile([P, 4, GROUPS, 4], F32, name="scores")
+            src = s_bank[r, s][:].rearrange("p (m j hh hl) -> p j hl m hh", j=4, hh=4, hl=4)
+            ms = slice(s * GROUPS_PER_BANK, (s + 1) * GROUPS_PER_BANK)
+            for j in range(4):
+                rows = slice(j * QUAD, (j + 1) * QUAD)
+                nc.scalar.copy(out=scores[r][rows, :, ms, :], in_=src[rows, j])
+
+        def transpose_scores(r):
+            bank = next_bank()
+            for hl in range(4):
+                nc.tensor.transpose(bank[:, hl * P:(hl + 1) * P],
+                                    scores[r][:, hl].rearrange("p m hh -> p (m hh)"), ident[:])
+            soft[r, "bank"] = bank[:].rearrange("p (c g) -> p c g", g=H)
+
+        def row_max(r):
+            top = stage.tile([P, BANK // H], F32, name="top")
+            nc.vector.tensor_reduce(out=top[:], in_=soft[r, "bank"], axis=AX.X, op=ALU.max)
+            soft[r, "top"] = top
+
+        def shift(r):
+            shifted = stage.tile([P, BANK // H, H], F32, name="shifted")
+            nc.vector.tensor_tensor(out=shifted[:], in0=soft[r, "bank"],
+                                    in1=soft[r, "top"][:].unsqueeze(2).to_broadcast([P, BANK // H, H]),
+                                    op=ALU.subtract)
+            soft[r, "shifted"] = shifted
+
+        def exponentiate(r):
+            expd = stage.tile([P, BANK // H, H], F32, name="expd")
+            nc.scalar.activation(out=expd[:], in_=soft[r, "shifted"][:], func=ACT.Exp, scale=HD ** -0.5)
+            soft[r, "expd"] = expd
+
+        def row_sum(r):
+            total = stage.tile([P, BANK // H], F32, name="total")
+            nc.vector.tensor_reduce(out=total[:], in_=soft[r, "expd"][:], axis=AX.X, op=ALU.add)
+            soft[r, "total"] = total
+
+        def invert(r):
+            inverse = stage.tile([P, BANK // H], F32, name="inverse")
+            nc.vector.reciprocal(out=inverse[:], in_=soft[r, "total"][:])
+            soft[r, "inverse"] = inverse
+
+        def normalise_and_store(r):
+            result = stage.tile([P, 4, 2, 4, H], F32, name="result")
+            nc.vector.tensor_tensor(
+                out=result[:].rearrange("p j a hl g -> p (j a) hl g"),
+                in0=soft[r, "expd"][:].rearrange("p (hl ja) g -> p ja hl g", hl=4),
+                in1=soft[r, "inverse"][:].rearrange("p (hl ja) -> p ja hl", hl=4).unsqueeze(3).to_broadcast([P, 8, 4, H]),
+                op=ALU.mult)
+            for a in range(2):
+                rows = out_rows[(2 * r + a) * P:(2 * r + a + 1) * P, :]
+                nc.sync.dma_start(out=rows.rearrange("(j m) (hh e) -> (m hh) j e", j=4, hh=4),
+                                  in_=result[:, :, a].rearrange("p j hl g -> p j (hl g)"))
+
+        def project_and_empty(t, b):
+            project(t, b)
+            empty_projection(t, b)
+
+        def turn_heads(r, s):
+            transpose_heads(r, s)
+            empty_heads(r, s)
+
+        make_identity(nc, ident[:])
+        nc.vector.memset(q_bias_rows[:], 0.0)
+        for buf in k_masked:
+            nc.vector.memset(buf[:], 0.0)
+        load_x(0)
+        load_w(0)
+        load_x(1)
+        load_w(1)
+        for c in range(2, 5):
+            load_x(2 * c - 2)
+            load_x(2 * c - 1)
+            load_w(c)
+        nc.sync.dma_start(out=k_bias[:], in_=b_qk[D:2 * D].partition_broadcast(P))
+        for c in range(5, CHUNKS):
+            load_w(c)
+        for a in range(2):
+            nc.sync.dma_start(out=q_bias_rows[0:H, a, :], in_=b_qk[0:D].rearrange("(h d) -> h d", d=HD))
+
+        for t in (0, 1):
+            transpose_x(t)
+            empty_x(t)
+        quantize_x(0)
+        interleave_w(0, nc.vector.tensor_copy)
+        quantize_x(1)
+        interleave_w(1, nc.scalar.copy)
+        quantize_w(0)
+        for t in (2, 3):
+            transpose_x(t)
+            empty_x(t)
+        interleave_w(2, nc.vector.tensor_copy)
+        quantize_w(1)
+        quantize_x(2)
+        quantize_x(3)
+        quantize_w(2)
+        for t in (0, 1):
+            project_and_empty(t, 0)
+        for t in (4, 5):
+            transpose_x(t)
+            empty_x(t)
+        interleave_w(3, nc.vector.tensor_copy)
+        quantize_x(4)
+        quantize_x(5)
+        quantize_w(3)
+        for t in (2, 3):
+            project_and_empty(t, 0)
+        for t in (6, 7):
+            transpose_x(t)
+            empty_x(t)
+        interleave_w(4, nc.vector.tensor_copy)
+        quantize_x(6)
+        quantize_x(7)
+        quantize_w(4)
+        for t in range(4, TILES):
+            project_and_empty(t, 0)
+        interleave_w(5, nc.vector.tensor_copy)
+        interleave_w(6, nc.vector.tensor_copy)
+        quantize_w(5)
+        for t in range(TILES):
+            project_and_empty(t, 1)
+        interleave_w(7, nc.vector.tensor_copy)
+        quantize_w(6)
+        project_and_empty(0, 2)
+        quantize_w(7)
+        project_and_empty(1, 2)
+        project_and_empty(0, 3)
+        project_and_empty(1, 3)
+
+        nc.vector.tensor_copy(out=q_bias_rows32[:], in_=q_bias_rows[:].rearrange("p a d -> p (a d)"))
+        bias_bank = next_bank()
+        nc.tensor.transpose(bias_bank[:, 0:P], q_bias_rows32[:], ident[:])
+        nc.scalar.copy(out=q_bias[:], in_=bias_bank[:, 0:H])
+
+        for s in range(8):
+            turn_heads(0, s)
+
+        for r in range(PAIRS):
+            ahead = r + 1 < PAIRS
+            if ahead:
+                for b in range(Q_BLOCKS, BLOCKS):
+                    for a in range(2):
+                        project_and_empty(2 * (r + 1) + a, b)
+            for s in range(4):
+                score(r, s)
+                empty_scores(r, s)
+                if r > 0 and s == 0:
+                    row_sum(r - 1)
+                if ahead:
+                    turn_heads(r + 1, s)
+                    if r > 0 and s == 0:
+                        invert(r - 1)
+                    turn_heads(r + 1, 4 + s)
+                elif s == 0:
+                    invert(r - 1)
+                if r > 0 and s == 1:
+                    normalise_and_store(r - 1)
+            transpose_scores(r)
+            row_max(r)
+            shift(r)
+            exponentiate(r)
+        row_sum(PAIRS - 1)
+        invert(PAIRS - 1)
+        normalise_and_store(PAIRS - 1)

@@ -30,7 +30,11 @@ PAIRS = TILES // 2
 CHUNKS = BLOCKS * PASSES
 GROUPS = QUAD
 GROUPS_PER_BANK = 8
+ROWS = 8
+SLOTS = 4 * PAIRS
 PSUM_BANKS = 8
+BLOCK_ORDER = (0, 2, 1, 3)
+W_ORDER = tuple(b * PASSES + g for b in BLOCK_ORDER for g in range(PASSES))
 
 FLOPS = 2 * TOKENS * C * 2 * D + 2 * TOKENS * H * H * HD
 
@@ -64,9 +68,10 @@ def tile_attention_pa_kernel(tc, x, w_qk, b_qk, out):
         proj = [[keep.tile([P, HEADS_PER_BLOCK, 2, HD], F32, name="proj%d_%d" % (r, b)) for b in range(BLOCKS)]
                 for r in range(PAIRS)]
         k_masked = [keep.tile([P, GROUPS, 4, 2, H], F32, name="k_masked%d" % i) for i in range(2)]
-        k_bias = keep.tile([P, D], BF16, name="k_bias")
+        k_bias_row = keep.tile([P, D], BF16, name="k_bias_row")
+        k_bias = keep.tile([P, D], F32, name="k_bias")
+        ident_bf16 = keep.tile([P, H], BF16, name="ident_bf16")
         q_bias_rows = keep.tile([P, 2, HD], BF16, name="q_bias_rows")
-        q_bias_rows32 = keep.tile([P, 2 * HD], F32, name="q_bias_rows32")
         q_bias = keep.tile([P, H], F32, name="q_bias")
         x_grouped, w_grouped, x_bank, mx_bank = {}, {}, {}, {}
         q_moving, scores, t_bank, s_bank, soft = {}, {}, {}, {}, {}
@@ -90,7 +95,7 @@ def tile_attention_pa_kernel(tc, x, w_qk, b_qk, out):
                                         words[:, 2 * P * g + u:2 * P * (g + 1):2], ident[:])
 
         def empty_x(t):
-            grouped = stage.tile([P, PASSES * P * PACK], BF16, name="x_grouped", bufs=4, align_bytes=64)
+            grouped = stage.tile([P, PASSES * P * PACK], BF16, name="x_grouped", bufs=2, align_bytes=64)
             x_grouped[t] = grouped
             nc.scalar.copy(out=grouped[:].bitcast(F32).rearrange("p (g r u) -> p g r u", g=PASSES, u=2),
                            in_=x_bank[t][:].rearrange("p (g u r) -> p g r u", g=PASSES, u=2))
@@ -139,20 +144,23 @@ def tile_attention_pa_kernel(tc, x, w_qk, b_qk, out):
                                     proj[r][b][:, first + i, :, :].rearrange("p a d -> p (a d)"), ident[:])
             t_bank[r, s] = bank
 
-        def empty_heads(r, s):
-            src = t_bank[r, s][:].rearrange("p (h j m) -> p m j h", h=4, j=4)
-            if s < 4:
-                if s == 0:
-                    q_moving[r] = stage.tile([P, GROUPS, 4, H], F32, name="q_moving")
-                bias = q_bias[:, 4 * s:4 * s + 4].unsqueeze(1).unsqueeze(1).to_broadcast([P, GROUPS, 4, 4])
-                nc.vector.tensor_tensor(out=q_moving[r][:, :, :, 4 * s:4 * s + 4], in0=src, in1=bias, op=ALU.add)
-            else:
-                g0 = 4 * (s - 4)
-                for a in range(2):
-                    rows = slice(a * HALF, (a + 1) * HALF)
-                    nc.scalar.copy(out=k_masked[r % 2][rows, :, :, a, g0:g0 + 4], in_=src[rows])
+        def heads_by_token(r, s):
+            return t_bank[r, s][:].rearrange("p (h j m) -> p j m h", h=4, j=4)
 
-        def score(r, s):
+        def empty_queries(r, s):
+            if s == 0:
+                q_moving[r] = stage.tile([P, GROUPS, 4, H], F32, name="q_moving")
+            bias = q_bias[:, 4 * s:4 * s + 4].unsqueeze(1).unsqueeze(1).to_broadcast([P, 4, GROUPS, 4])
+            dst = q_moving[r][:, :, :, 4 * s:4 * s + 4].rearrange("p m j h -> p j m h")
+            nc.vector.tensor_tensor(out=dst, in0=heads_by_token(r, s), in1=bias, op=ALU.add)
+
+        def empty_keys(r, s, a, copy):
+            rows = slice(a * HALF, (a + 1) * HALF)
+            dst = k_masked[r % 2][rows, :, :, a, 4 * s:4 * s + 4].rearrange("p m j g -> p j m g")
+            copy(out=dst, in_=heads_by_token(r, 4 + s)[rows])
+
+        def score(n):
+            r, s = divmod(n, 4)
             bank = next_bank()
             for i in range(GROUPS_PER_BANK):
                 m = s * GROUPS_PER_BANK + i
@@ -160,170 +168,208 @@ def tile_attention_pa_kernel(tc, x, w_qk, b_qk, out):
                                  lhsT=k_masked[r % 2][:, m].rearrange("p j a g -> p (j a g)"),
                                  rhs=q_moving[r][:, m].rearrange("p j h -> p (j h)"),
                                  start=True, stop=True)
-            s_bank[r, s] = bank
+            s_bank[n] = bank
+            scores[n] = stage.tile([P, GROUPS_PER_BANK, H], F32, name="scores", bufs=3)
 
-        def empty_scores(r, s):
-            if s == 0:
-                scores[r] = stage.tile([P, 4, GROUPS, 4], F32, name="scores")
-            src = s_bank[r, s][:].rearrange("p (m j hh hl) -> p j hl m hh", j=4, hh=4, hl=4)
-            ms = slice(s * GROUPS_PER_BANK, (s + 1) * GROUPS_PER_BANK)
-            for j in range(4):
-                rows = slice(j * QUAD, (j + 1) * QUAD)
-                nc.scalar.copy(out=scores[r][rows, :, ms, :], in_=src[rows, j])
+        def pick_scores(n, j):
+            rows = slice(j * QUAD, (j + 1) * QUAD)
+            src = s_bank[n][:].rearrange("p (m j h) -> p j m h", j=4, h=H)
+            nc.scalar.copy(out=scores[n][rows], in_=src[rows, j])
 
-        def transpose_scores(r):
+        def transpose_scores(n):
             bank = next_bank()
-            for hl in range(4):
-                nc.tensor.transpose(bank[:, hl * P:(hl + 1) * P],
-                                    scores[r][:, hl].rearrange("p m hh -> p (m hh)"), ident[:])
-            soft[r, "bank"] = bank[:].rearrange("p (c g) -> p c g", g=H)
+            nc.tensor.transpose(bank[:, 0:P], scores[n][:].rearrange("p m h -> p (m h)"), ident[:])
+            soft[n, "bank"] = bank[:, 0:P].rearrange("p (c g) -> p c g", g=H)
 
-        def row_max(r):
-            top = stage.tile([P, BANK // H], F32, name="top")
-            nc.vector.tensor_reduce(out=top[:], in_=soft[r, "bank"], axis=AX.X, op=ALU.max)
-            soft[r, "top"] = top
+        def row_max(n):
+            top = stage.tile([P, ROWS], F32, name="top")
+            nc.vector.tensor_reduce(out=top[:], in_=soft[n, "bank"], axis=AX.X, op=ALU.max)
+            soft[n, "top"] = top
 
-        def shift(r):
-            shifted = stage.tile([P, BANK // H, H], F32, name="shifted")
-            nc.vector.tensor_tensor(out=shifted[:], in0=soft[r, "bank"],
-                                    in1=soft[r, "top"][:].unsqueeze(2).to_broadcast([P, BANK // H, H]),
+        def shift(n):
+            shifted = stage.tile([P, ROWS, H], F32, name="shifted")
+            nc.vector.tensor_tensor(out=shifted[:], in0=soft[n, "bank"],
+                                    in1=soft[n, "top"][:].unsqueeze(2).to_broadcast([P, ROWS, H]),
                                     op=ALU.subtract)
-            soft[r, "shifted"] = shifted
+            soft[n, "shifted"] = shifted
 
-        def exponentiate(r):
-            expd = stage.tile([P, BANK // H, H], F32, name="expd")
-            nc.scalar.activation(out=expd[:], in_=soft[r, "shifted"][:], func=ACT.Exp, scale=HD ** -0.5)
-            soft[r, "expd"] = expd
+        def exponentiate(n):
+            expd = stage.tile([P, ROWS, H], F32, name="expd")
+            nc.scalar.activation(out=expd[:], in_=soft[n, "shifted"][:], func=ACT.Exp, scale=HD ** -0.5)
+            soft[n, "expd"] = expd
 
-        def row_sum(r):
-            total = stage.tile([P, BANK // H], F32, name="total")
-            nc.vector.tensor_reduce(out=total[:], in_=soft[r, "expd"][:], axis=AX.X, op=ALU.add)
-            soft[r, "total"] = total
+        def row_sum(n):
+            total = stage.tile([P, ROWS], F32, name="total")
+            nc.vector.tensor_reduce(out=total[:], in_=soft[n, "expd"][:], axis=AX.X, op=ALU.add)
+            soft[n, "total"] = total
 
-        def invert(r):
-            inverse = stage.tile([P, BANK // H], F32, name="inverse")
-            nc.vector.reciprocal(out=inverse[:], in_=soft[r, "total"][:])
-            soft[r, "inverse"] = inverse
+        def invert(n):
+            inverse = stage.tile([P, ROWS], F32, name="inverse")
+            nc.vector.reciprocal(out=inverse[:], in_=soft[n, "total"][:])
+            soft[n, "inverse"] = inverse
 
-        def normalise_and_store(r):
-            result = stage.tile([P, 4, 2, 4, H], F32, name="result")
+        def normalise_and_store(n):
+            r, s = divmod(n, 4)
+            result = stage.tile([P, 2, 4, H], F32, name="result", bufs=4)
             nc.vector.tensor_tensor(
-                out=result[:].rearrange("p j a hl g -> p (j a) hl g"),
-                in0=soft[r, "expd"][:].rearrange("p (hl ja) g -> p ja hl g", hl=4),
-                in1=soft[r, "inverse"][:].rearrange("p (hl ja) -> p ja hl", hl=4).unsqueeze(3).to_broadcast([P, 8, 4, H]),
+                out=result[:].rearrange("p a j g -> p j a g"),
+                in0=soft[n, "expd"][:].rearrange("p (j a) g -> p j a g", a=2),
+                in1=soft[n, "inverse"][:].rearrange("p (j a) -> p j a", a=2).unsqueeze(3).to_broadcast([P, 4, 2, H]),
                 op=ALU.mult)
-            for a in range(2):
-                rows = out_rows[(2 * r + a) * P:(2 * r + a + 1) * P, :]
-                nc.sync.dma_start(out=rows.rearrange("(j m) (hh e) -> (m hh) j e", j=4, hh=4),
-                                  in_=result[:, :, a].rearrange("p j hl g -> p j (hl g)"))
+            rows = out_rows[2 * r * P:2 * (r + 1) * P, :].rearrange("(c s m) (h g) -> s (m h) c g", s=4, m=8, g=H)
+            nc.sync.dma_start(out=rows[s], in_=result[:].rearrange("p a j g -> p (a j) g"))
 
         def project_and_empty(t, b):
             project(t, b)
             empty_projection(t, b)
 
-        def turn_heads(r, s):
-            transpose_heads(r, s)
-            empty_heads(r, s)
-
         make_identity(nc, ident[:])
         nc.vector.memset(q_bias_rows[:], 0.0)
+        nc.vector.memset(k_bias_row[:], 0.0)
+        for a in range(2):
+            nc.scalar.dma_start(out=q_bias_rows[0:H, a, :], in_=b_qk[0:D].rearrange("(h d) -> h d", d=HD))
+        nc.scalar.dma_start(out=k_bias_row[0:1, :], in_=b_qk[D:2 * D].rearrange("(o n) -> o n", o=1))
         for buf in k_masked:
             nc.vector.memset(buf[:], 0.0)
         load_x(0)
         load_w(0)
         load_x(1)
-        load_w(1)
-        for c in range(2, 5):
-            load_x(2 * c - 2)
-            load_x(2 * c - 1)
+        for c in W_ORDER[1:]:
             load_w(c)
-        nc.sync.dma_start(out=k_bias[:], in_=b_qk[D:2 * D].partition_broadcast(P))
-        for c in range(5, CHUNKS):
-            load_w(c)
-        for a in range(2):
-            nc.sync.dma_start(out=q_bias_rows[0:H, a, :], in_=b_qk[0:D].rearrange("(h d) -> h d", d=HD))
+        for t in range(2, TILES):
+            load_x(t)
 
-        for t in (0, 1):
+        def spread_biases():
+            nc.scalar.copy(out=ident_bf16[:], in_=ident[:, 0:H])
+            bank = next_bank()
+            nc.tensor.matmul(bank[:, 0:H], lhsT=q_bias_rows[:].rearrange("p a d -> p (a d)"), rhs=ident_bf16[:],
+                             start=True, stop=True)
+            nc.scalar.copy(out=q_bias[:], in_=bank[:, 0:H])
+            for i in range(D // BANK):
+                cols = slice(i * BANK, (i + 1) * BANK)
+                bank = next_bank()
+                nc.tensor.matmul(bank[:], lhsT=ident_bf16[:, 0:1].to_broadcast([P, P]), rhs=k_bias_row[:, cols],
+                                 start=True, stop=True)
+                nc.scalar.copy(out=k_bias[:, cols], in_=bank[:])
+
+        def turn_x(t):
             transpose_x(t)
             empty_x(t)
+
+        def project_pair(r, i):
+            for a in range(2):
+                project_and_empty(2 * r + a, BLOCK_ORDER[i])
+
+        def turn_queries(r, s):
+            transpose_heads(r, s)
+            empty_queries(r, s)
+
+        def turn_keys(r, s, second_copy):
+            transpose_heads(r, 4 + s)
+            empty_keys(r, s, 0, nc.scalar.copy)
+            empty_keys(r, s, 1, second_copy)
+
+        on_vector, on_scalar = nc.vector.tensor_copy, nc.scalar.copy
+        w = W_ORDER
+        spread_biases()
+        turn_x(0)
+        interleave_w(w[0], on_vector)
         quantize_x(0)
-        interleave_w(0, nc.vector.tensor_copy)
+        turn_x(1)
+        quantize_w(w[0])
+        interleave_w(w[1], on_scalar)
         quantize_x(1)
-        interleave_w(1, nc.scalar.copy)
-        quantize_w(0)
-        for t in (2, 3):
-            transpose_x(t)
-            empty_x(t)
-        interleave_w(2, nc.vector.tensor_copy)
-        quantize_w(1)
+        interleave_w(w[2], on_vector)
+        quantize_w(w[1])
+        interleave_w(w[3], on_scalar)
+        quantize_w(w[2])
+        project_pair(0, 0)
+        interleave_w(w[4], on_vector)
+        quantize_w(w[3])
+        interleave_w(w[5], on_scalar)
+        project_pair(0, 1)
+        quantize_w(w[4])
+        interleave_w(w[6], on_vector)
+        transpose_heads(0, 4)
+        transpose_heads(0, 5)
+        for a in range(2):
+            empty_keys(0, 0, a, on_scalar)
+            empty_keys(0, 1, a, on_scalar)
+        quantize_w(w[5])
+        interleave_w(w[7], on_vector)
+        project_pair(0, 2)
+        quantize_w(w[6])
+        turn_queries(0, 0)
+        quantize_w(w[7])
+        turn_x(2)
+        turn_x(3)
+        turn_queries(0, 1)
+        project_pair(0, 3)
         quantize_x(2)
         quantize_x(3)
-        quantize_w(2)
-        for t in (0, 1):
-            project_and_empty(t, 0)
-        for t in (4, 5):
-            transpose_x(t)
-            empty_x(t)
-        interleave_w(3, nc.vector.tensor_copy)
+        turn_queries(0, 2)
+        transpose_heads(0, 6)
+        transpose_heads(0, 7)
+        empty_keys(0, 2, 0, on_scalar)
+        empty_keys(0, 3, 1, on_vector)
+        empty_keys(0, 2, 1, on_scalar)
+        empty_keys(0, 3, 0, on_vector)
+        project_and_empty(2, 0)
+        turn_queries(0, 3)
+        project_and_empty(2, 2)
+        project_and_empty(3, 0)
+        project_and_empty(3, 2)
+        turn_x(4)
+        project(2, 1)
+        project(2, 3)
         quantize_x(4)
-        quantize_x(5)
-        quantize_w(3)
-        for t in (2, 3):
-            project_and_empty(t, 0)
-        for t in (6, 7):
-            transpose_x(t)
-            empty_x(t)
-        interleave_w(4, nc.vector.tensor_copy)
-        quantize_x(6)
-        quantize_x(7)
-        quantize_w(4)
-        for t in range(4, TILES):
-            project_and_empty(t, 0)
-        interleave_w(5, nc.vector.tensor_copy)
-        interleave_w(6, nc.vector.tensor_copy)
-        quantize_w(5)
-        for t in range(TILES):
-            project_and_empty(t, 1)
-        interleave_w(7, nc.vector.tensor_copy)
-        quantize_w(6)
-        project_and_empty(0, 2)
-        quantize_w(7)
-        project_and_empty(1, 2)
-        project_and_empty(0, 3)
-        project_and_empty(1, 3)
 
-        nc.vector.tensor_copy(out=q_bias_rows32[:], in_=q_bias_rows[:].rearrange("p a d -> p (a d)"))
-        bias_bank = next_bank()
-        nc.tensor.transpose(bias_bank[:, 0:P], q_bias_rows32[:], ident[:])
-        nc.scalar.copy(out=q_bias[:], in_=bias_bank[:, 0:H])
+        def in_range(n):
+            return 0 <= n < SLOTS
 
-        for s in range(8):
-            turn_heads(0, s)
+        def projected_in(n):
+            r, i = divmod(n + 7, 4)
+            return (2 * r + i % 2, i // 2) if r < PAIRS else None
 
-        for r in range(PAIRS):
-            ahead = r + 1 < PAIRS
-            if ahead:
-                for b in range(Q_BLOCKS, BLOCKS):
-                    for a in range(2):
-                        project_and_empty(2 * (r + 1) + a, b)
-            for s in range(4):
-                score(r, s)
-                empty_scores(r, s)
-                if r > 0 and s == 0:
-                    row_sum(r - 1)
-                if ahead:
-                    turn_heads(r + 1, s)
-                    if r > 0 and s == 0:
-                        invert(r - 1)
-                    turn_heads(r + 1, 4 + s)
-                elif s == 0:
-                    invert(r - 1)
-                if r > 0 and s == 1:
-                    normalise_and_store(r - 1)
-            transpose_scores(r)
-            row_max(r)
-            shift(r)
-            exponentiate(r)
-        row_sum(PAIRS - 1)
-        invert(PAIRS - 1)
-        normalise_and_store(PAIRS - 1)
+        for n in range(SLOTS + 3):
+            r_turn, i_turn = divmod(n + 4, 4)
+            r_x, i_x = divmod(n + 9, 4)
+            turning = r_turn < PAIRS
+            loading = r_x < PAIRS and i_x < 2
+            if projected_in(n - 1):
+                t, b = projected_in(n - 1)
+                empty_projection(t, b)
+                empty_projection(t, Q_BLOCKS + b)
+            if in_range(n - 1):
+                for j in range(4):
+                    pick_scores(n - 1, j)
+            if in_range(n - 3):
+                row_sum(n - 3)
+            if in_range(n - 2):
+                transpose_scores(n - 2)
+                row_max(n - 2)
+            if in_range(n - 3):
+                invert(n - 3)
+            if turning:
+                transpose_heads(r_turn, 4 + i_turn)
+                transpose_heads(r_turn, i_turn)
+            if in_range(n - 2):
+                shift(n - 2)
+            if in_range(n - 3):
+                normalise_and_store(n - 3)
+            if turning:
+                empty_queries(r_turn, i_turn)
+                for a in range(2):
+                    empty_keys(r_turn, i_turn, a, on_scalar)
+            if in_range(n - 2):
+                exponentiate(n - 2)
+            if loading:
+                turn_x(2 * r_x + i_x)
+            if in_range(n):
+                score(n)
+            if loading:
+                quantize_x(2 * r_x + i_x)
+            if projected_in(n):
+                t, b = projected_in(n)
+                project(t, b)
+                project(t, Q_BLOCKS + b)

from contextlib import ExitStack

import concourse.mybir as mybir
from concourse.masks import make_identity

F32 = mybir.dt.float32
BF16 = mybir.dt.bfloat16
U32 = mybir.dt.uint32
U8 = mybir.dt.uint8
E4M3X4 = mybir.dt.float8_e4m3fn_x4
E5M2X4 = mybir.dt.float8_e5m2_x4
ALU = mybir.AluOpType
ACT = mybir.ActivationFunctionType
AX = mybir.AxisListType

TOKENS, C, D, H = 1024, 1024, 1024, 16
HD = D // H
P = 128
HALF = P // 2
QUAD = P // 4
PACK = 4
K_PASS = P * PACK
PASSES = C // K_PASS
BANK = 512
BLOCKS = 2 * D // BANK
Q_BLOCKS = BLOCKS // 2
HEADS_PER_BLOCK = BANK // HD
TILES = TOKENS // P
PAIRS = TILES // 2
CHUNKS = BLOCKS * PASSES
GROUPS = QUAD
GROUPS_PER_BANK = 8
ROWS = 8
SLOTS = 4 * PAIRS
PSUM_BANKS = 8
BLOCK_ORDER = (0, 2, 1, 3)
W_ORDER = tuple(b * PASSES + g for b in BLOCK_ORDER for g in range(PASSES))

FLOPS = 2 * TOKENS * C * 2 * D + 2 * TOKENS * H * H * HD


def tile_attention_pa_kernel(tc, x, w_qk, b_qk, out):
    nc = tc.nc
    x_rows = x.rearrange("n t c -> (n t) c")
    out_rows = out.rearrange("n t h g -> (n t) (h g)")

    with ExitStack() as ctx:
        keep = ctx.enter_context(tc.tile_pool(name="keep", bufs=1))
        stage = ctx.enter_context(tc.tile_pool(name="stage", bufs=2))
        psum = ctx.enter_context(tc.psum_pool(name="psum", bufs=1))
        ctx.enter_context(tc.manual_schedule())

        banks_taken = []

        def next_bank():
            index = len(banks_taken) % PSUM_BANKS
            bank = psum.tile([P, BANK], F32, name="bank%d" % index)
            banks_taken.append(index)
            return bank

        ident = keep.tile([P, P], F32, name="ident")
        x_raw = [keep.tile([P, C], BF16, name="x_raw%d" % t) for t in range(TILES)]
        w_raw = [keep.tile([P, PACK, BANK], BF16, name="w_raw%d" % c) for c in range(CHUNKS)]
        x_codes = [keep.tile([P, PASSES * P], U32, name="x_codes%d" % t, align_bytes=64) for t in range(TILES)]
        x_scales = [keep.tile([P, PASSES * P], U8, name="x_scales%d" % t, align_bytes=64) for t in range(TILES)]
        w_codes = [keep.tile([P, BANK], U32, name="w_codes%d" % c, align_bytes=64) for c in range(CHUNKS)]
        w_scales = [keep.tile([P, BANK], U8, name="w_scales%d" % c, align_bytes=64) for c in range(CHUNKS)]
        proj = [[keep.tile([P, HEADS_PER_BLOCK, 2, HD], F32, name="proj%d_%d" % (r, b)) for b in range(BLOCKS)]
                for r in range(PAIRS)]
        k_masked = [keep.tile([P, GROUPS, 4, 2, H], F32, name="k_masked%d" % i) for i in range(2)]
        k_bias_row = keep.tile([P, D], BF16, name="k_bias_row")
        k_bias = keep.tile([P, D], F32, name="k_bias")
        ident_bf16 = keep.tile([P, H], BF16, name="ident_bf16")
        q_bias_rows = keep.tile([P, 2, HD], BF16, name="q_bias_rows")
        q_bias = keep.tile([P, H], F32, name="q_bias")
        x_grouped, w_grouped, x_bank, mx_bank = {}, {}, {}, {}
        q_moving, scores, t_bank, s_bank, soft = {}, {}, {}, {}, {}

        def load_x(t):
            nc.sync.dma_start(out=x_raw[t][:], in_=x_rows[t * P:(t + 1) * P, :])

        def load_w(c):
            b, g = divmod(c, PASSES)
            rows = w_qk[g * K_PASS:(g + 1) * K_PASS, b * BANK:(b + 1) * BANK]
            nc.sync.dma_start(out=w_raw[c][:], in_=rows.rearrange("(p j) n -> p j n", j=PACK))

        def transpose_x(t):
            words = x_raw[t][:].bitcast(F32)
            bank = next_bank()
            x_bank[t] = bank
            for g in range(PASSES):
                for u in range(2):
                    slot = 2 * g + u
                    nc.tensor.transpose(bank[:, slot * P:(slot + 1) * P],
                                        words[:, 2 * P * g + u:2 * P * (g + 1):2], ident[:])

        def empty_x(t):
            grouped = stage.tile([P, PASSES * P * PACK], BF16, name="x_grouped", bufs=2, align_bytes=64)
            x_grouped[t] = grouped
            nc.scalar.copy(out=grouped[:].bitcast(F32).rearrange("p (g r u) -> p g r u", g=PASSES, u=2),
                           in_=x_bank[t][:].rearrange("p (g u r) -> p g r u", g=PASSES, u=2))

        def quantize_x(t):
            nc.vector.quantize_mx(out=x_codes[t][:].bitcast(E5M2X4), scales=x_scales[t][:], in_=x_grouped[t][:])

        def interleave_w(c, copy):
            grouped = stage.tile([P, BANK * PACK], BF16, name="w_grouped", bufs=3, align_bytes=64)
            w_grouped[c] = grouped
            copy(out=grouped[:].rearrange("p (c i t) -> p c t i", i=4, t=PACK),
                 in_=w_raw[c][:].rearrange("p t (c i) -> p c t i", i=4))

        def quantize_w(c):
            nc.vector.quantize_mx(out=w_codes[c][:].bitcast(E4M3X4), scales=w_scales[c][:], in_=w_grouped[c][:])

        def project(t, b):
            bank = next_bank()
            for g in range(PASSES):
                c = b * PASSES + g
                nc.tensor.matmul_mx(
                    out=bank[:],
                    lhsT=x_codes[t][:, g * P:(g + 1) * P].bitcast(E5M2X4),
                    lhsT_scale=x_scales[t][:, g * P:(g + 1) * P],
                    rhs=w_codes[c][:].bitcast(E4M3X4),
                    rhs_scale=w_scales[c][:],
                    start=(g == 0), stop=(g == PASSES - 1))
            mx_bank[t, b] = bank

        def empty_projection(t, b):
            r, a = divmod(t, 2)
            src = mx_bank[t, b][:].rearrange("p (h d) -> p h d", d=HD)
            dst = proj[r][b][:, :, a, :]
            if b < Q_BLOCKS:
                nc.scalar.copy(out=dst, in_=src)
            else:
                cols = slice((b - Q_BLOCKS) * BANK, (b - Q_BLOCKS + 1) * BANK)
                nc.vector.tensor_tensor(out=dst, in0=src, in1=k_bias[:, cols].rearrange("p (h d) -> p h d", d=HD),
                                        op=ALU.add)

        def transpose_heads(r, s):
            bank = next_bank()
            b, first = divmod(4 * s, HEADS_PER_BLOCK)
            for i in range(4):
                nc.tensor.transpose(bank[:, i * P:(i + 1) * P],
                                    proj[r][b][:, first + i, :, :].rearrange("p a d -> p (a d)"), ident[:])
            t_bank[r, s] = bank

        def heads_by_token(r, s):
            return t_bank[r, s][:].rearrange("p (h j m) -> p j m h", h=4, j=4)

        def empty_queries(r, s):
            if s == 0:
                q_moving[r] = stage.tile([P, GROUPS, 4, H], F32, name="q_moving")
            bias = q_bias[:, 4 * s:4 * s + 4].unsqueeze(1).unsqueeze(1).to_broadcast([P, 4, GROUPS, 4])
            dst = q_moving[r][:, :, :, 4 * s:4 * s + 4].rearrange("p m j h -> p j m h")
            nc.vector.tensor_tensor(out=dst, in0=heads_by_token(r, s), in1=bias, op=ALU.add)

        def empty_keys(r, s, a, copy):
            rows = slice(a * HALF, (a + 1) * HALF)
            dst = k_masked[r % 2][rows, :, :, a, 4 * s:4 * s + 4].rearrange("p m j g -> p j m g")
            copy(out=dst, in_=heads_by_token(r, 4 + s)[rows])

        def score(n):
            r, s = divmod(n, 4)
            bank = next_bank()
            for i in range(GROUPS_PER_BANK):
                m = s * GROUPS_PER_BANK + i
                nc.tensor.matmul(bank[:, i * 4 * H:(i + 1) * 4 * H],
                                 lhsT=k_masked[r % 2][:, m].rearrange("p j a g -> p (j a g)"),
                                 rhs=q_moving[r][:, m].rearrange("p j h -> p (j h)"),
                                 start=True, stop=True)
            s_bank[n] = bank
            scores[n] = stage.tile([P, GROUPS_PER_BANK, H], F32, name="scores", bufs=3)

        def pick_scores(n, j):
            rows = slice(j * QUAD, (j + 1) * QUAD)
            src = s_bank[n][:].rearrange("p (m j h) -> p j m h", j=4, h=H)
            nc.scalar.copy(out=scores[n][rows], in_=src[rows, j])

        def transpose_scores(n):
            bank = next_bank()
            nc.tensor.transpose(bank[:, 0:P], scores[n][:].rearrange("p m h -> p (m h)"), ident[:])
            soft[n, "bank"] = bank[:, 0:P].rearrange("p (c g) -> p c g", g=H)

        def row_max(n):
            top = stage.tile([P, ROWS], F32, name="top")
            nc.vector.tensor_reduce(out=top[:], in_=soft[n, "bank"], axis=AX.X, op=ALU.max)
            soft[n, "top"] = top

        def shift(n):
            shifted = stage.tile([P, ROWS, H], F32, name="shifted")
            nc.vector.tensor_tensor(out=shifted[:], in0=soft[n, "bank"],
                                    in1=soft[n, "top"][:].unsqueeze(2).to_broadcast([P, ROWS, H]),
                                    op=ALU.subtract)
            soft[n, "shifted"] = shifted

        def exponentiate(n):
            expd = stage.tile([P, ROWS, H], F32, name="expd")
            nc.scalar.activation(out=expd[:], in_=soft[n, "shifted"][:], func=ACT.Exp, scale=HD ** -0.5)
            soft[n, "expd"] = expd

        def row_sum(n):
            total = stage.tile([P, ROWS], F32, name="total")
            nc.vector.tensor_reduce(out=total[:], in_=soft[n, "expd"][:], axis=AX.X, op=ALU.add)
            soft[n, "total"] = total

        def invert(n):
            inverse = stage.tile([P, ROWS], F32, name="inverse")
            nc.vector.reciprocal(out=inverse[:], in_=soft[n, "total"][:])
            soft[n, "inverse"] = inverse

        def normalise_and_store(n):
            r, s = divmod(n, 4)
            result = stage.tile([P, 2, 4, H], F32, name="result", bufs=4)
            nc.vector.tensor_tensor(
                out=result[:].rearrange("p a j g -> p j a g"),
                in0=soft[n, "expd"][:].rearrange("p (j a) g -> p j a g", a=2),
                in1=soft[n, "inverse"][:].rearrange("p (j a) -> p j a", a=2).unsqueeze(3).to_broadcast([P, 4, 2, H]),
                op=ALU.mult)
            rows = out_rows[2 * r * P:2 * (r + 1) * P, :].rearrange("(c s m) (h g) -> s (m h) c g", s=4, m=8, g=H)
            nc.sync.dma_start(out=rows[s], in_=result[:].rearrange("p a j g -> p (a j) g"))

        def project_and_empty(t, b):
            project(t, b)
            empty_projection(t, b)

        make_identity(nc, ident[:])
        nc.vector.memset(q_bias_rows[:], 0.0)
        nc.vector.memset(k_bias_row[:], 0.0)
        for a in range(2):
            nc.scalar.dma_start(out=q_bias_rows[0:H, a, :], in_=b_qk[0:D].rearrange("(h d) -> h d", d=HD))
        nc.scalar.dma_start(out=k_bias_row[0:1, :], in_=b_qk[D:2 * D].rearrange("(o n) -> o n", o=1))
        for buf in k_masked:
            nc.vector.memset(buf[:], 0.0)
        load_x(0)
        load_w(0)
        load_x(1)
        for c in W_ORDER[1:]:
            load_w(c)
        for t in range(2, TILES):
            load_x(t)

        def spread_biases():
            nc.scalar.copy(out=ident_bf16[:], in_=ident[:, 0:H])
            bank = next_bank()
            nc.tensor.matmul(bank[:, 0:H], lhsT=q_bias_rows[:].rearrange("p a d -> p (a d)"), rhs=ident_bf16[:],
                             start=True, stop=True)
            nc.scalar.copy(out=q_bias[:], in_=bank[:, 0:H])
            for i in range(D // BANK):
                cols = slice(i * BANK, (i + 1) * BANK)
                bank = next_bank()
                nc.tensor.matmul(bank[:], lhsT=ident_bf16[:, 0:1].to_broadcast([P, P]), rhs=k_bias_row[:, cols],
                                 start=True, stop=True)
                nc.scalar.copy(out=k_bias[:, cols], in_=bank[:])

        def turn_x(t):
            transpose_x(t)
            empty_x(t)

        def project_pair(r, i):
            for a in range(2):
                project_and_empty(2 * r + a, BLOCK_ORDER[i])

        def turn_queries(r, s):
            transpose_heads(r, s)
            empty_queries(r, s)

        def turn_keys(r, s, second_copy):
            transpose_heads(r, 4 + s)
            empty_keys(r, s, 0, nc.scalar.copy)
            empty_keys(r, s, 1, second_copy)

        on_vector, on_scalar = nc.vector.tensor_copy, nc.scalar.copy
        w = W_ORDER
        spread_biases()
        turn_x(0)
        interleave_w(w[0], on_vector)
        quantize_x(0)
        turn_x(1)
        quantize_w(w[0])
        interleave_w(w[1], on_scalar)
        quantize_x(1)
        interleave_w(w[2], on_vector)
        quantize_w(w[1])
        interleave_w(w[3], on_scalar)
        quantize_w(w[2])
        project_pair(0, 0)
        interleave_w(w[4], on_vector)
        quantize_w(w[3])
        interleave_w(w[5], on_scalar)
        project_pair(0, 1)
        quantize_w(w[4])
        interleave_w(w[6], on_vector)
        transpose_heads(0, 4)
        transpose_heads(0, 5)
        for a in range(2):
            empty_keys(0, 0, a, on_scalar)
            empty_keys(0, 1, a, on_scalar)
        quantize_w(w[5])
        interleave_w(w[7], on_vector)
        project_pair(0, 2)
        quantize_w(w[6])
        turn_queries(0, 0)
        quantize_w(w[7])
        turn_x(2)
        turn_x(3)
        turn_queries(0, 1)
        project_pair(0, 3)
        quantize_x(2)
        quantize_x(3)
        turn_queries(0, 2)
        transpose_heads(0, 6)
        transpose_heads(0, 7)
        empty_keys(0, 2, 0, on_scalar)
        empty_keys(0, 3, 1, on_vector)
        empty_keys(0, 2, 1, on_scalar)
        empty_keys(0, 3, 0, on_vector)
        project_and_empty(2, 0)
        turn_queries(0, 3)
        project_and_empty(2, 2)
        project_and_empty(3, 0)
        project_and_empty(3, 2)
        turn_x(4)
        project(2, 1)
        project(2, 3)
        quantize_x(4)

        def in_range(n):
            return 0 <= n < SLOTS

        def projected_in(n):
            r, i = divmod(n + 7, 4)
            return (2 * r + i % 2, i // 2) if r < PAIRS else None

        for n in range(SLOTS + 3):
            r_turn, i_turn = divmod(n + 4, 4)
            r_x, i_x = divmod(n + 9, 4)
            turning = r_turn < PAIRS
            loading = r_x < PAIRS and i_x < 2
            if projected_in(n - 1):
                t, b = projected_in(n - 1)
                empty_projection(t, b)
                empty_projection(t, Q_BLOCKS + b)
            if in_range(n - 1):
                for j in range(4):
                    pick_scores(n - 1, j)
            if in_range(n - 3):
                row_sum(n - 3)
            if in_range(n - 2):
                transpose_scores(n - 2)
                row_max(n - 2)
            if in_range(n - 3):
                invert(n - 3)
            if turning:
                transpose_heads(r_turn, 4 + i_turn)
                transpose_heads(r_turn, i_turn)
            if in_range(n - 2):
                shift(n - 2)
            if in_range(n - 3):
                normalise_and_store(n - 3)
            if turning:
                empty_queries(r_turn, i_turn)
                for a in range(2):
                    empty_keys(r_turn, i_turn, a, on_scalar)
            if in_range(n - 2):
                exponentiate(n - 2)
            if loading:
                turn_x(2 * r_x + i_x)
            if in_range(n):
                score(n)
            if loading:
                quantize_x(2 * r_x + i_x)
            if projected_in(n):
                t, b = projected_in(n)
                project(t, b)
                project(t, Q_BLOCKS + b)
